import numpy as np
import ml_dtypes

BF16 = ml_dtypes.bfloat16


def bf(x):
    return np.asarray(x, np.float32).astype(BF16)


def f32(x):
    return np.asarray(x, np.float32)


def f64(x):
    return np.asarray(x).astype(np.float64)


def striped(idx):
    return np.tile(idx.reshape(-1, 16).T, (8, 1))


C, S, N, D = 256, 512, 384, 256


def setup_inputs():
    return {"x": bf(np.random.standard_normal((D, C))), "rw": bf(np.random.standard_normal((D, N)) / np.sqrt(D)), "rb": f32(0.2 * np.random.standard_normal((1, N))), "base": f32(np.random.standard_normal((C, S))), "offs": striped(np.random.permutation(S)[:N])}


def reference(x, rw, rb, base, offs):
    idx = offs[:16].T.reshape(-1)
    out = f64(base).copy()
    out[:, idx] = np.tanh(f64(x).T @ f64(rw) + f64(rb))
    return out

@@ -1,0 +1,60 @@
+import concourse.mybir as mybir
+
+P = 128
+D, C, N, S = 256, 256, 384, 512
+D_BLOCKS = D // P
+C_BLOCKS = C // P
+
+FLOPS = 2 * C * D * N
+
+BF16, F32, U16 = mybir.dt.bfloat16, mybir.dt.float32, mybir.dt.uint16
+ADD = mybir.AluOpType.add
+TANH = mybir.ActivationFunctionType.Tanh
+COPY = mybir.ActivationFunctionType.Copy
+
+
+def tile_godareamodel_kernel(tc, x, rw, rb, base, offs, out):
+    nc = tc.nc
+    with (
+        tc.tile_pool(name="held", bufs=1) as held,
+        tc.tile_pool(name="work", bufs=2) as work,
+        tc.psum_pool(name="psum", bufs=2) as psum,
+    ):
+        x_blocks = []
+        rw_blocks = []
+        for k in range(D_BLOCKS):
+            x_block = held.tile([P, C], BF16, name=f"x_block{k}")
+            nc.sync.dma_start(x_block[:], x[k * P : (k + 1) * P, :])
+            x_blocks.append(x_block)
+            rw_block = held.tile([P, N], BF16, name=f"rw_block{k}")
+            nc.scalar.dma_start(rw_block[:], rw[k * P : (k + 1) * P, :])
+            rw_blocks.append(rw_block)
+
+        bias = held.tile([P, N], F32, name="bias")
+        nc.gpsimd.dma_start(bias[:], rb.squeeze(0).partition_broadcast(P))
+
+        offsets = held.tile([P, N // 16], U16, name="offsets")
+        nc.sync.dma_start(offsets[:], offs)
+
+        windows = []
+        for c in range(C_BLOCKS):
+            window = held.tile([P, S], F32, name=f"window{c}")
+            nc.sync.dma_start(window[:], base[c * P : (c + 1) * P, :])
+            windows.append(window)
+
+        for c in range(C_BLOCKS):
+            acc = psum.tile([P, N], F32, name="acc")
+            for k in range(D_BLOCKS):
+                nc.tensor.matmul(
+                    acc[:],
+                    x_blocks[k][:, c * P : (c + 1) * P],
+                    rw_blocks[k][:],
+                    start=(k == 0),
+                    stop=(k == D_BLOCKS - 1),
+                )
+            biased = work.tile([P, N], F32, name="biased")
+            nc.vector.tensor_tensor(biased[:], acc[:], bias[:], ADD)
+            values = work.tile([P, N], F32, name="values")
+            nc.scalar.activation(values[:], biased[:], TANH)
+            nc.scalar.activation(windows[c][:].indirect(offsets[:]), values[:], COPY)
+            nc.sync.dma_start(out[c * P : (c + 1) * P, :], windows[c][:])

@@ -31,7 +31,7 @@ def tile_godareamodel_kernel(tc, x, rw, rb, base, offs, out):
             rw_blocks.append(rw_block)
 
         bias = held.tile([P, N], F32, name="bias")
-        nc.gpsimd.dma_start(bias[:], rb.squeeze(0).partition_broadcast(P))
+        nc.scalar.dma_start(bias[:], rb.squeeze(0).partition_broadcast(P))
 
         offsets = held.tile([P, N // 16], U16, name="offsets")
         nc.sync.dma_start(offsets[:], offs)

@@ -4,6 +4,8 @@ P = 128
 D, C, N, S = 256, 256, 384, 512
 D_BLOCKS = D // P
 C_BLOCKS = C // P
+HALVES = 2
+H = N // HALVES
 
 FLOPS = 2 * C * D * N
 
@@ -18,43 +20,42 @@ def tile_godareamodel_kernel(tc, x, rw, rb, base, offs, out):
     with (
         tc.tile_pool(name="held", bufs=1) as held,
         tc.tile_pool(name="work", bufs=2) as work,
-        tc.psum_pool(name="psum", bufs=2) as psum,
+        tc.tile_pool(name="single", bufs=1) as single,
+        tc.psum_pool(name="psum", bufs=C_BLOCKS * HALVES) as psum,
     ):
-        x_blocks = []
-        rw_blocks = []
-        for k in range(D_BLOCKS):
-            x_block = held.tile([P, C], BF16, name=f"x_block{k}")
-            nc.sync.dma_start(x_block[:], x[k * P : (k + 1) * P, :])
-            x_blocks.append(x_block)
-            rw_block = held.tile([P, N], BF16, name=f"rw_block{k}")
-            nc.scalar.dma_start(rw_block[:], rw[k * P : (k + 1) * P, :])
-            rw_blocks.append(rw_block)
-
-        bias = held.tile([P, N], F32, name="bias")
-        nc.scalar.dma_start(bias[:], rb.squeeze(0).partition_broadcast(P))
-
+        x_tile = held.tile([P, D_BLOCKS, C], BF16, name="x_tile")
+        rw_halves = [held.tile([P, D_BLOCKS, H], BF16, name=f"rw_half{h}") for h in range(HALVES)]
+        bias_halves = [held.tile([P, H], F32, name=f"bias_half{h}") for h in range(HALVES)]
         offsets = held.tile([P, N // 16], U16, name="offsets")
+        windows = [held.tile([P, S], F32, name=f"window{c}") for c in range(C_BLOCKS)]
+
+        x_view = x.rearrange("(k p) c -> p k c", p=P)
+        rw_view = rw.rearrange("(k p) n -> p k n", p=P)
+        bias_views = [rb[:, h * H : (h + 1) * H].squeeze(0).partition_broadcast(P) for h in range(HALVES)]
+
+        nc.sync.dma_start(x_tile[:], x_view)
+        nc.scalar.dma_start(rw_halves[0][:], rw_view[:, :, 0:H])
+        nc.sync.dma_start(bias_halves[0][:], bias_views[0])
+        nc.scalar.dma_start(rw_halves[1][:], rw_view[:, :, H:N])
+        nc.scalar.dma_start(bias_halves[1][:], bias_views[1])
         nc.sync.dma_start(offsets[:], offs)
-
-        windows = []
-        for c in range(C_BLOCKS):
-            window = held.tile([P, S], F32, name=f"window{c}")
-            nc.sync.dma_start(window[:], base[c * P : (c + 1) * P, :])
-            windows.append(window)
+        nc.sync.dma_start(windows[0][:], base[0:P, :])
+        nc.sync.dma_start(windows[1][:], base[P : 2 * P, :])
 
         for c in range(C_BLOCKS):
-            acc = psum.tile([P, N], F32, name="acc")
-            for k in range(D_BLOCKS):
-                nc.tensor.matmul(
-                    acc[:],
-                    x_blocks[k][:, c * P : (c + 1) * P],
-                    rw_blocks[k][:],
-                    start=(k == 0),
-                    stop=(k == D_BLOCKS - 1),
-                )
-            biased = work.tile([P, N], F32, name="biased")
-            nc.vector.tensor_tensor(biased[:], acc[:], bias[:], ADD)
-            values = work.tile([P, N], F32, name="values")
-            nc.scalar.activation(values[:], biased[:], TANH)
+            values = single.tile([P, N], F32, name="values")
+            for h in range(HALVES):
+                acc = psum.tile([P, H], F32, name="acc")
+                for k in range(D_BLOCKS):
+                    nc.tensor.matmul(
+                        acc[:],
+                        x_tile[:, k, c * P : (c + 1) * P],
+                        rw_halves[h][:, k, :],
+                        start=(k == 0),
+                        stop=(k == D_BLOCKS - 1),
+                    )
+                biased = work.tile([P, H], F32, name="biased")
+                nc.vector.tensor_tensor(biased[:], acc[:], bias_halves[h][:], ADD)
+                nc.scalar.activation(values[:, h * H : (h + 1) * H], biased[:], TANH)
             nc.scalar.activation(windows[c][:].indirect(offsets[:]), values[:], COPY)
             nc.sync.dma_start(out[c * P : (c + 1) * P, :], windows[c][:])

@@ -4,8 +4,6 @@ P = 128
 D, C, N, S = 256, 256, 384, 512
 D_BLOCKS = D // P
 C_BLOCKS = C // P
-HALVES = 2
-H = N // HALVES
 
 FLOPS = 2 * C * D * N
 
@@ -20,42 +18,36 @@ def tile_godareamodel_kernel(tc, x, rw, rb, base, offs, out):
     with (
         tc.tile_pool(name="held", bufs=1) as held,
         tc.tile_pool(name="work", bufs=2) as work,
-        tc.tile_pool(name="single", bufs=1) as single,
-        tc.psum_pool(name="psum", bufs=C_BLOCKS * HALVES) as psum,
+        tc.psum_pool(name="psum", bufs=2) as psum,
     ):
-        x_tile = held.tile([P, D_BLOCKS, C], BF16, name="x_tile")
-        rw_halves = [held.tile([P, D_BLOCKS, H], BF16, name=f"rw_half{h}") for h in range(HALVES)]
-        bias_halves = [held.tile([P, H], F32, name=f"bias_half{h}") for h in range(HALVES)]
+        x_blocks = [held.tile([P, C], BF16, name=f"x_block{k}") for k in range(D_BLOCKS)]
+        rw_blocks = [held.tile([P, N], BF16, name=f"rw_block{k}") for k in range(D_BLOCKS)]
+        bias = held.tile([P, N], F32, name="bias")
         offsets = held.tile([P, N // 16], U16, name="offsets")
         windows = [held.tile([P, S], F32, name=f"window{c}") for c in range(C_BLOCKS)]
 
-        x_view = x.rearrange("(k p) c -> p k c", p=P)
-        rw_view = rw.rearrange("(k p) n -> p k n", p=P)
-        bias_views = [rb[:, h * H : (h + 1) * H].squeeze(0).partition_broadcast(P) for h in range(HALVES)]
+        nc.scalar.dma_start(bias[:], rb.squeeze(0).partition_broadcast(P))
+        nc.scalar.dma_start(windows[1][:], base[P : 2 * P, :])
 
-        nc.sync.dma_start(x_tile[:], x_view)
-        nc.scalar.dma_start(rw_halves[0][:], rw_view[:, :, 0:H])
-        nc.sync.dma_start(bias_halves[0][:], bias_views[0])
-        nc.scalar.dma_start(rw_halves[1][:], rw_view[:, :, H:N])
-        nc.scalar.dma_start(bias_halves[1][:], bias_views[1])
+        for k in range(D_BLOCKS):
+            nc.sync.dma_start(x_blocks[k][:], x[k * P : (k + 1) * P, :])
+            nc.sync.dma_start(rw_blocks[k][:], rw[k * P : (k + 1) * P, :])
         nc.sync.dma_start(offsets[:], offs)
         nc.sync.dma_start(windows[0][:], base[0:P, :])
-        nc.sync.dma_start(windows[1][:], base[P : 2 * P, :])
 
         for c in range(C_BLOCKS):
-            values = single.tile([P, N], F32, name="values")
-            for h in range(HALVES):
-                acc = psum.tile([P, H], F32, name="acc")
-                for k in range(D_BLOCKS):
-                    nc.tensor.matmul(
-                        acc[:],
-                        x_tile[:, k, c * P : (c + 1) * P],
-                        rw_halves[h][:, k, :],
-                        start=(k == 0),
-                        stop=(k == D_BLOCKS - 1),
-                    )
-                biased = work.tile([P, H], F32, name="biased")
-                nc.vector.tensor_tensor(biased[:], acc[:], bias_halves[h][:], ADD)
-                nc.scalar.activation(values[:, h * H : (h + 1) * H], biased[:], TANH)
+            acc = psum.tile([P, N], F32, name="acc")
+            for k in range(D_BLOCKS):
+                nc.tensor.matmul(
+                    acc[:],
+                    x_blocks[k][:, c * P : (c + 1) * P],
+                    rw_blocks[k][:],
+                    start=(k == 0),
+                    stop=(k == D_BLOCKS - 1),
+                )
+            biased = work.tile([P, N], F32, name="biased")
+            nc.vector.tensor_tensor(biased[:], acc[:], bias[:], ADD)
+            values = work.tile([P, N], F32, name="values")
+            nc.scalar.activation(values[:], biased[:], TANH)
             nc.scalar.activation(windows[c][:].indirect(offsets[:]), values[:], COPY)
             nc.sync.dma_start(out[c * P : (c + 1) * P, :], windows[c][:])

@@ -4,6 +4,8 @@ P = 128
 D, C, N, S = 256, 256, 384, 512
 D_BLOCKS = D // P
 C_BLOCKS = C // P
+HALVES = 2
+H = N // HALVES
 
 FLOPS = 2 * C * D * N
 
@@ -17,37 +19,47 @@ def tile_godareamodel_kernel(tc, x, rw, rb, base, offs, out):
     nc = tc.nc
     with (
         tc.tile_pool(name="held", bufs=1) as held,
-        tc.tile_pool(name="work", bufs=2) as work,
-        tc.psum_pool(name="psum", bufs=2) as psum,
+        tc.tile_pool(name="work", bufs=C_BLOCKS) as work,
+        tc.tile_pool(name="pieces", bufs=C_BLOCKS * HALVES) as pieces,
+        tc.psum_pool(name="psum", bufs=C_BLOCKS * HALVES) as psum,
     ):
-        x_blocks = [held.tile([P, C], BF16, name=f"x_block{k}") for k in range(D_BLOCKS)]
-        rw_blocks = [held.tile([P, N], BF16, name=f"rw_block{k}") for k in range(D_BLOCKS)]
-        bias = held.tile([P, N], F32, name="bias")
-        offsets = held.tile([P, N // 16], U16, name="offsets")
-        windows = [held.tile([P, S], F32, name=f"window{c}") for c in range(C_BLOCKS)]
-
-        nc.scalar.dma_start(bias[:], rb.squeeze(0).partition_broadcast(P))
-        nc.scalar.dma_start(windows[1][:], base[P : 2 * P, :])
-
+        x_blocks = []
+        rw_blocks = []
         for k in range(D_BLOCKS):
-            nc.sync.dma_start(x_blocks[k][:], x[k * P : (k + 1) * P, :])
-            nc.sync.dma_start(rw_blocks[k][:], rw[k * P : (k + 1) * P, :])
+            x_block = held.tile([P, C], BF16, name=f"x_block{k}")
+            nc.sync.dma_start(x_block[:], x[k * P : (k + 1) * P, :])
+            x_blocks.append(x_block)
+            rw_block = held.tile([P, N], BF16, name=f"rw_block{k}")
+            nc.scalar.dma_start(rw_block[:], rw[k * P : (k + 1) * P, :])
+            rw_blocks.append(rw_block)
+
+        bias = held.tile([P, N], F32, name="bias")
+        nc.scalar.dma_start(bias[:], rb.squeeze(0).partition_broadcast(P))
+
+        offsets = held.tile([P, N // 16], U16, name="offsets")
         nc.sync.dma_start(offsets[:], offs)
-        nc.sync.dma_start(windows[0][:], base[0:P, :])
+
+        windows = []
+        for c in range(C_BLOCKS):
+            window = held.tile([P, S], F32, name=f"window{c}")
+            nc.sync.dma_start(window[:], base[c * P : (c + 1) * P, :])
+            windows.append(window)
 
         for c in range(C_BLOCKS):
-            acc = psum.tile([P, N], F32, name="acc")
-            for k in range(D_BLOCKS):
-                nc.tensor.matmul(
-                    acc[:],
-                    x_blocks[k][:, c * P : (c + 1) * P],
-                    rw_blocks[k][:],
-                    start=(k == 0),
-                    stop=(k == D_BLOCKS - 1),
-                )
-            biased = work.tile([P, N], F32, name="biased")
-            nc.vector.tensor_tensor(biased[:], acc[:], bias[:], ADD)
             values = work.tile([P, N], F32, name="values")
-            nc.scalar.activation(values[:], biased[:], TANH)
+            for h in range(HALVES):
+                half = slice(h * H, (h + 1) * H)
+                acc = psum.tile([P, H], F32, name="acc")
+                for k in range(D_BLOCKS):
+                    nc.tensor.matmul(
+                        acc[:],
+                        x_blocks[k][:, c * P : (c + 1) * P],
+                        rw_blocks[k][:, half],
+                        start=(k == 0),
+                        stop=(k == D_BLOCKS - 1),
+                    )
+                biased = pieces.tile([P, H], F32, name="biased")
+                nc.vector.tensor_tensor(biased[:], acc[:], bias[:, half], ADD)
+                nc.scalar.activation(values[:, half], biased[:], TANH)
             nc.scalar.activation(windows[c][:].indirect(offsets[:]), values[:], COPY)
             nc.sync.dma_start(out[c * P : (c + 1) * P, :], windows[c][:])

@@ -6,6 +6,8 @@ D_BLOCKS = D // P
 C_BLOCKS = C // P
 HALVES = 2
 H = N // HALVES
+BANK = 512
+WARM_UPS = 3
 
 FLOPS = 2 * C * D * N
 
@@ -22,28 +24,26 @@ def tile_godareamodel_kernel(tc, x, rw, rb, base, offs, out):
         tc.tile_pool(name="work", bufs=C_BLOCKS) as work,
         tc.tile_pool(name="pieces", bufs=C_BLOCKS * HALVES) as pieces,
         tc.psum_pool(name="psum", bufs=C_BLOCKS * HALVES) as psum,
+        tc.psum_pool(name="idle", bufs=1) as idle,
     ):
-        x_blocks = []
-        rw_blocks = []
-        for k in range(D_BLOCKS):
-            x_block = held.tile([P, C], BF16, name=f"x_block{k}")
-            nc.sync.dma_start(x_block[:], x[k * P : (k + 1) * P, :])
-            x_blocks.append(x_block)
-            rw_block = held.tile([P, N], BF16, name=f"rw_block{k}")
-            nc.scalar.dma_start(rw_block[:], rw[k * P : (k + 1) * P, :])
-            rw_blocks.append(rw_block)
+        zeros = held.tile([P, BANK], BF16, name="zeros")
+        nc.vector.memset(zeros[:], 0.0)
+        unread = idle.tile([P, BANK], F32, name="unread")
+        for warm_up in range(WARM_UPS):
+            nc.tensor.matmul(unread[:], zeros[:, 0:P], zeros[:], start=True, stop=True)
 
+        x_tile = held.tile([P, D_BLOCKS, C], BF16, name="x_tile")
+        rw_tile = held.tile([P, D_BLOCKS, N], BF16, name="rw_tile")
         bias = held.tile([P, N], F32, name="bias")
-        nc.scalar.dma_start(bias[:], rb.squeeze(0).partition_broadcast(P))
-
         offsets = held.tile([P, N // 16], U16, name="offsets")
-        nc.sync.dma_start(offsets[:], offs)
+        windows = [held.tile([P, S], F32, name=f"window{c}") for c in range(C_BLOCKS)]
 
-        windows = []
-        for c in range(C_BLOCKS):
-            window = held.tile([P, S], F32, name=f"window{c}")
-            nc.sync.dma_start(window[:], base[c * P : (c + 1) * P, :])
-            windows.append(window)
+        nc.sync.dma_start(x_tile[:], x.rearrange("(k p) c -> p k c", p=P))
+        nc.scalar.dma_start(rw_tile[:], rw.rearrange("(k p) n -> p k n", p=P))
+        nc.scalar.dma_start(bias[:], rb.squeeze(0).partition_broadcast(P))
+        nc.sync.dma_start(offsets[:], offs)
+        nc.sync.dma_start(windows[0][:], base[0:P, :])
+        nc.scalar.dma_start(windows[1][:], base[P : 2 * P, :])
 
         for c in range(C_BLOCKS):
             values = work.tile([P, N], F32, name="values")
@@ -53,8 +53,8 @@ def tile_godareamodel_kernel(tc, x, rw, rb, base, offs, out):
                 for k in range(D_BLOCKS):
                     nc.tensor.matmul(
                         acc[:],
-                        x_blocks[k][:, c * P : (c + 1) * P],
-                        rw_blocks[k][:, half],
+                        x_tile[:, k, c * P : (c + 1) * P],
+                        rw_tile[:, k, half],
                         start=(k == 0),
                         stop=(k == D_BLOCKS - 1),
                     )

@@ -6,8 +6,6 @@ D_BLOCKS = D // P
 C_BLOCKS = C // P
 HALVES = 2
 H = N // HALVES
-BANK = 512
-WARM_UPS = 3
 
 FLOPS = 2 * C * D * N
 
@@ -24,14 +22,7 @@ def tile_godareamodel_kernel(tc, x, rw, rb, base, offs, out):
         tc.tile_pool(name="work", bufs=C_BLOCKS) as work,
         tc.tile_pool(name="pieces", bufs=C_BLOCKS * HALVES) as pieces,
         tc.psum_pool(name="psum", bufs=C_BLOCKS * HALVES) as psum,
-        tc.psum_pool(name="idle", bufs=1) as idle,
     ):
-        zeros = held.tile([P, BANK], BF16, name="zeros")
-        nc.vector.memset(zeros[:], 0.0)
-        unread = idle.tile([P, BANK], F32, name="unread")
-        for warm_up in range(WARM_UPS):
-            nc.tensor.matmul(unread[:], zeros[:, 0:P], zeros[:], start=True, stop=True)
-
         x_tile = held.tile([P, D_BLOCKS, C], BF16, name="x_tile")
         rw_tile = held.tile([P, D_BLOCKS, N], BF16, name="rw_tile")
         bias = held.tile([P, N], F32, name="bias")

@@ -6,6 +6,8 @@ D_BLOCKS = D // P
 C_BLOCKS = C // P
 HALVES = 2
 H = N // HALVES
+BANK = 512
+WARM_UPS = 3
 
 FLOPS = 2 * C * D * N
 
@@ -22,7 +24,14 @@ def tile_godareamodel_kernel(tc, x, rw, rb, base, offs, out):
         tc.tile_pool(name="work", bufs=C_BLOCKS) as work,
         tc.tile_pool(name="pieces", bufs=C_BLOCKS * HALVES) as pieces,
         tc.psum_pool(name="psum", bufs=C_BLOCKS * HALVES) as psum,
+        tc.psum_pool(name="idle", bufs=1) as idle,
     ):
+        zeros = held.tile([P, BANK], BF16, name="zeros")
+        nc.vector.memset(zeros[:], 0.0)
+        unread = idle.tile([P, BANK], F32, name="unread")
+        for warm_up in range(WARM_UPS):
+            nc.tensor.matmul(unread[:], zeros[:, 0:P], zeros[:], start=True, stop=True)
+
         x_tile = held.tile([P, D_BLOCKS, C], BF16, name="x_tile")
         rw_tile = held.tile([P, D_BLOCKS, N], BF16, name="rw_tile")
         bias = held.tile([P, N], F32, name="bias")
@@ -31,10 +40,10 @@ def tile_godareamodel_kernel(tc, x, rw, rb, base, offs, out):
 
         nc.sync.dma_start(x_tile[:], x.rearrange("(k p) c -> p k c", p=P))
         nc.scalar.dma_start(rw_tile[:], rw.rearrange("(k p) n -> p k n", p=P))
-        nc.scalar.dma_start(bias[:], rb.squeeze(0).partition_broadcast(P))
         nc.sync.dma_start(offsets[:], offs)
-        nc.sync.dma_start(windows[0][:], base[0:P, :])
-        nc.scalar.dma_start(windows[1][:], base[P : 2 * P, :])
+        nc.scalar.dma_start(bias[:], rb.squeeze(0).partition_broadcast(P))
+        for c in range(C_BLOCKS):
+            nc.scalar.dma_start(windows[c][:], base[c * P : (c + 1) * P, :])
 
         for c in range(C_BLOCKS):
             values = work.tile([P, N], F32, name="values")

@@ -61,5 +61,9 @@ def tile_godareamodel_kernel(tc, x, rw, rb, base, offs, out):
                 biased = pieces.tile([P, H], F32, name="biased")
                 nc.vector.tensor_tensor(biased[:], acc[:], bias[:, half], ADD)
                 nc.scalar.activation(values[:, half], biased[:], TANH)
-            nc.scalar.activation(windows[c][:].indirect(offsets[:]), values[:], COPY)
+                nc.scalar.activation(
+                    windows[c][:].indirect(offsets[:, h * H // 16 : (h + 1) * H // 16]),
+                    values[:, half],
+                    COPY,
+                )
             nc.sync.dma_start(out[c * P : (c + 1) * P, :], windows[c][:])

@@ -1,18 +1,15 @@
 import concourse.mybir as mybir
+from concourse.masks import make_identity
 
 P = 128
 D, C, N, S = 256, 256, 384, 512
-D_BLOCKS = D // P
-C_BLOCKS = C // P
-HALVES = 2
-H = N // HALVES
+D_BLOCKS, C_BLOCKS, N_BLOCKS = D // P, C // P, N // P
 BANK = 512
 WARM_UPS = 3
 
 FLOPS = 2 * C * D * N
 
 BF16, F32, U16 = mybir.dt.bfloat16, mybir.dt.float32, mybir.dt.uint16
-ADD = mybir.AluOpType.add
 TANH = mybir.ActivationFunctionType.Tanh
 COPY = mybir.ActivationFunctionType.Copy
 
@@ -21,9 +18,10 @@ def tile_godareamodel_kernel(tc, x, rw, rb, base, offs, out):
     nc = tc.nc
     with (
         tc.tile_pool(name="held", bufs=1) as held,
-        tc.tile_pool(name="work", bufs=C_BLOCKS) as work,
-        tc.tile_pool(name="pieces", bufs=C_BLOCKS * HALVES) as pieces,
-        tc.psum_pool(name="psum", bufs=C_BLOCKS * HALVES) as psum,
+        tc.tile_pool(name="work", bufs=N_BLOCKS) as work,
+        tc.tile_pool(name="pieces", bufs=N_BLOCKS * C_BLOCKS) as pieces,
+        tc.psum_pool(name="sums", bufs=N_BLOCKS) as sums,
+        tc.psum_pool(name="flips", bufs=4) as flips,
         tc.psum_pool(name="idle", bufs=1) as idle,
     ):
         zeros = held.tile([P, BANK], BF16, name="zeros")
@@ -34,36 +32,49 @@ def tile_godareamodel_kernel(tc, x, rw, rb, base, offs, out):
 
         x_tile = held.tile([P, D_BLOCKS, C], BF16, name="x_tile")
         rw_tile = held.tile([P, D_BLOCKS, N], BF16, name="rw_tile")
-        bias = held.tile([P, N], F32, name="bias")
+        bias = held.tile([P, N_BLOCKS], F32, name="bias")
         offsets = held.tile([P, N // 16], U16, name="offsets")
         windows = [held.tile([P, S], F32, name=f"window{c}") for c in range(C_BLOCKS)]
+        identity = held.tile([P, P], F32, name="identity")
+        make_identity(nc, identity[:])
 
         nc.sync.dma_start(x_tile[:], x.rearrange("(k p) c -> p k c", p=P))
         nc.scalar.dma_start(rw_tile[:], rw.rearrange("(k p) n -> p k n", p=P))
+        nc.sync.dma_start(bias[:], rb.rearrange("o (b p) -> p (o b)", p=P))
         nc.sync.dma_start(offsets[:], offs)
-        nc.scalar.dma_start(bias[:], rb.squeeze(0).partition_broadcast(P))
         for c in range(C_BLOCKS):
             nc.scalar.dma_start(windows[c][:], base[c * P : (c + 1) * P, :])
 
-        for c in range(C_BLOCKS):
-            values = work.tile([P, N], F32, name="values")
-            for h in range(HALVES):
-                half = slice(h * H, (h + 1) * H)
-                acc = psum.tile([P, H], F32, name="acc")
-                for k in range(D_BLOCKS):
-                    nc.tensor.matmul(
-                        acc[:],
-                        x_tile[:, k, c * P : (c + 1) * P],
-                        rw_tile[:, k, half],
-                        start=(k == 0),
-                        stop=(k == D_BLOCKS - 1),
-                    )
-                biased = pieces.tile([P, H], F32, name="biased")
-                nc.vector.tensor_tensor(biased[:], acc[:], bias[:, half], ADD)
-                nc.scalar.activation(values[:, half], biased[:], TANH)
+        early = held.tile([P, 1], F32, name="early")
+        nc.gpsimd.memset(early[:], 0.0)
+        unused = held.tile([P, 1], F32, name="unused")
+        nc.scalar.activation(unused[:], early[:], TANH)
+
+        finished = []
+        for b in range(N_BLOCKS):
+            acc = sums.tile([P, C], F32, name="acc")
+            for k in range(D_BLOCKS):
+                nc.tensor.matmul(
+                    acc[:],
+                    rw_tile[:, k, b * P : (b + 1) * P],
+                    x_tile[:, k, :],
+                    start=(k == 0),
+                    stop=(k == D_BLOCKS - 1),
+                )
+            values = work.tile([P, C], F32, name="values")
+            nc.scalar.activation(values[:], acc[:], TANH, bias=bias[:, b : b + 1])
+            finished.append(values)
+
+        for b in range(N_BLOCKS):
+            for c in range(C_BLOCKS):
+                flip = flips.tile([P, P], F32, name="flip")
+                nc.tensor.transpose(flip[:], finished[b][:, c * P : (c + 1) * P], identity[:])
+                piece = pieces.tile([P, P], F32, name="piece")
+                nc.vector.tensor_copy(piece[:], flip[:])
                 nc.scalar.activation(
-                    windows[c][:].indirect(offsets[:, h * H // 16 : (h + 1) * H // 16]),
-                    values[:, half],
+                    windows[c][:].indirect(offsets[:, b * P // 16 : (b + 1) * P // 16]),
+                    piece[:],
                     COPY,
                 )
+        for c in range(C_BLOCKS):
             nc.sync.dma_start(out[c * P : (c + 1) * P, :], windows[c][:])

@@ -5,7 +5,7 @@ P = 128
 D, C, N, S = 256, 256, 384, 512
 D_BLOCKS, C_BLOCKS, N_BLOCKS = D // P, C // P, N // P
 BANK = 512
-WARM_UPS = 3
+WARM_UPS = 2
 
 FLOPS = 2 * C * D * N
 
@@ -18,10 +18,10 @@ def tile_godareamodel_kernel(tc, x, rw, rb, base, offs, out):
     nc = tc.nc
     with (
         tc.tile_pool(name="held", bufs=1) as held,
-        tc.tile_pool(name="work", bufs=N_BLOCKS) as work,
+        tc.tile_pool(name="work", bufs=N_BLOCKS * C_BLOCKS) as work,
         tc.tile_pool(name="pieces", bufs=N_BLOCKS * C_BLOCKS) as pieces,
-        tc.psum_pool(name="sums", bufs=N_BLOCKS) as sums,
-        tc.psum_pool(name="flips", bufs=4) as flips,
+        tc.psum_pool(name="sums", bufs=4) as sums,
+        tc.psum_pool(name="flips", bufs=3) as flips,
         tc.psum_pool(name="idle", bufs=1) as idle,
     ):
         zeros = held.tile([P, BANK], BF16, name="zeros")
@@ -38,9 +38,9 @@ def tile_godareamodel_kernel(tc, x, rw, rb, base, offs, out):
         identity = held.tile([P, P], F32, name="identity")
         make_identity(nc, identity[:])
 
-        nc.sync.dma_start(x_tile[:], x.rearrange("(k p) c -> p k c", p=P))
         nc.scalar.dma_start(rw_tile[:], rw.rearrange("(k p) n -> p k n", p=P))
         nc.sync.dma_start(bias[:], rb.rearrange("o (b p) -> p (o b)", p=P))
+        nc.sync.dma_start(x_tile[:], x.rearrange("(k p) c -> p k c", p=P))
         nc.sync.dma_start(offsets[:], offs)
         for c in range(C_BLOCKS):
             nc.scalar.dma_start(windows[c][:], base[c * P : (c + 1) * P, :])
@@ -50,31 +50,32 @@ def tile_godareamodel_kernel(tc, x, rw, rb, base, offs, out):
         unused = held.tile([P, 1], F32, name="unused")
         nc.scalar.activation(unused[:], early[:], TANH)
 
-        finished = []
         for b in range(N_BLOCKS):
-            acc = sums.tile([P, C], F32, name="acc")
-            for k in range(D_BLOCKS):
-                nc.tensor.matmul(
-                    acc[:],
-                    rw_tile[:, k, b * P : (b + 1) * P],
-                    x_tile[:, k, :],
-                    start=(k == 0),
-                    stop=(k == D_BLOCKS - 1),
-                )
-            values = work.tile([P, C], F32, name="values")
-            nc.scalar.activation(values[:], acc[:], TANH, bias=bias[:, b : b + 1])
-            finished.append(values)
-
-        for b in range(N_BLOCKS):
-            for c in range(C_BLOCKS):
-                flip = flips.tile([P, P], F32, name="flip")
-                nc.tensor.transpose(flip[:], finished[b][:, c * P : (c + 1) * P], identity[:])
-                piece = pieces.tile([P, P], F32, name="piece")
-                nc.vector.tensor_copy(piece[:], flip[:])
-                nc.scalar.activation(
-                    windows[c][:].indirect(offsets[:, b * P // 16 : (b + 1) * P // 16]),
-                    piece[:],
-                    COPY,
-                )
+            neurons = slice(b * P, (b + 1) * P)
+            width = P if b == 0 else C
+            for start in range(0, C, width):
+                acc = sums.tile([P, width], F32, name="acc")
+                for k in range(D_BLOCKS):
+                    nc.tensor.matmul(
+                        acc[:],
+                        rw_tile[:, k, neurons],
+                        x_tile[:, k, start : start + width],
+                        start=(k == 0),
+                        stop=(k == D_BLOCKS - 1),
+                    )
+                values = work.tile([P, width], F32, name="values")
+                nc.scalar.activation(values[:], acc[:], TANH, bias=bias[:, b : b + 1])
+                for c in range(start // P, (start + width) // P):
+                    flip = flips.tile([P, P], F32, name="flip")
+                    nc.tensor.transpose(
+                        flip[:], values[:, c * P - start : (c + 1) * P - start], identity[:]
+                    )
+                    piece = pieces.tile([P, P], F32, name="piece")
+                    nc.vector.tensor_copy(piece[:], flip[:])
+                    nc.scalar.activation(
+                        windows[c][:].indirect(offsets[:, b * P // 16 : (b + 1) * P // 16]),
+                        piece[:],
+                        COPY,
+                    )
         for c in range(C_BLOCKS):
             nc.sync.dma_start(out[c * P : (c + 1) * P, :], windows[c][:])

@@ -3,6 +3,7 @@ from concourse.masks import make_identity
 
 P = 128
 D, C, N, S = 256, 256, 384, 512
+BLOCK = 32
 D_BLOCKS, C_BLOCKS, N_BLOCKS = D // P, C // P, N // P
 BANK = 512
 WARM_UPS = 2
@@ -24,6 +25,9 @@ def tile_godareamodel_kernel(tc, x, rw, rb, base, offs, out):
         tc.psum_pool(name="flips", bufs=3) as flips,
         tc.psum_pool(name="idle", bufs=1) as idle,
     ):
+        bias_rows = held.tile([P, P], F32, name="bias_rows", align_bytes=64)
+        nc.vector.memset(bias_rows[:], 0.0)
+
         zeros = held.tile([P, BANK], BF16, name="zeros")
         nc.vector.memset(zeros[:], 0.0)
         unread = idle.tile([P, BANK], F32, name="unread")
@@ -32,18 +36,22 @@ def tile_godareamodel_kernel(tc, x, rw, rb, base, offs, out):
 
         x_tile = held.tile([P, D_BLOCKS, C], BF16, name="x_tile")
         rw_tile = held.tile([P, D_BLOCKS, N], BF16, name="rw_tile")
-        bias = held.tile([P, N_BLOCKS], F32, name="bias")
+        bias = held.tile([P, P], F32, name="bias", align_bytes=64)
         offsets = held.tile([P, N // 16], U16, name="offsets")
         windows = [held.tile([P, S], F32, name=f"window{c}") for c in range(C_BLOCKS)]
         identity = held.tile([P, P], F32, name="identity")
         make_identity(nc, identity[:])
 
-        nc.scalar.dma_start(rw_tile[:], rw.rearrange("(k p) n -> p k n", p=P))
-        nc.sync.dma_start(bias[:], rb.rearrange("o (b p) -> p (o b)", p=P))
         nc.sync.dma_start(x_tile[:], x.rearrange("(k p) c -> p k c", p=P))
+        nc.scalar.dma_start(rw_tile[:], rw.rearrange("(k p) n -> p k n", p=P))
+        nc.sync.dma_start(
+            bias_rows[0:P:BLOCK, 0 : N_BLOCKS * BLOCK],
+            rb.rearrange("o (b q i) -> q (o b) i", q=P // BLOCK, i=BLOCK),
+        )
+        nc.vector.transpose(bias[:], bias_rows[:])
         nc.sync.dma_start(offsets[:], offs)
         for c in range(C_BLOCKS):
-            nc.scalar.dma_start(windows[c][:], base[c * P : (c + 1) * P, :])
+            nc.sync.dma_start(windows[c][:], base[c * P : (c + 1) * P, :])
 
         early = held.tile([P, 1], F32, name="early")
         nc.gpsimd.memset(early[:], 0.0)
@@ -64,7 +72,7 @@ def tile_godareamodel_kernel(tc, x, rw, rb, base, offs, out):
                         stop=(k == D_BLOCKS - 1),
                     )
                 values = work.tile([P, width], F32, name="values")
-                nc.scalar.activation(values[:], acc[:], TANH, bias=bias[:, b : b + 1])
+                nc.scalar.activation(values[:], acc[:], TANH, bias=bias[:, b * BLOCK : b * BLOCK + 1])
                 for c in range(start // P, (start + width) // P):
                     flip = flips.tile([P, P], F32, name="flip")
                     nc.tensor.transpose(

@@ -42,8 +42,8 @@ def tile_godareamodel_kernel(tc, x, rw, rb, base, offs, out):
         identity = held.tile([P, P], F32, name="identity")
         make_identity(nc, identity[:])
 
-        nc.sync.dma_start(x_tile[:], x.rearrange("(k p) c -> p k c", p=P))
-        nc.scalar.dma_start(rw_tile[:], rw.rearrange("(k p) n -> p k n", p=P))
+        nc.sync.dma_start(x_tile[:], x.rearrange("(p k) c -> p k c", p=P))
+        nc.scalar.dma_start(rw_tile[:], rw.rearrange("(p k) n -> p k n", p=P))
         nc.sync.dma_start(
             bias_rows[0:P:BLOCK, 0 : N_BLOCKS * BLOCK],
             rb.rearrange("o (b q i) -> q (o b) i", q=P // BLOCK, i=BLOCK),

@@ -6,6 +6,7 @@ D, C, N, S = 256, 256, 384, 512
 BLOCK = 32
 D_BLOCKS, C_BLOCKS, N_BLOCKS = D // P, C // P, N // P
 BANK = 512
+GROUPS = ((0,), tuple(range(1, N_BLOCKS)))
 WARM_UPS = 2
 
 FLOPS = 2 * C * D * N
@@ -19,8 +20,8 @@ def tile_godareamodel_kernel(tc, x, rw, rb, base, offs, out):
     nc = tc.nc
     with (
         tc.tile_pool(name="held", bufs=1) as held,
-        tc.tile_pool(name="work", bufs=N_BLOCKS * C_BLOCKS) as work,
-        tc.tile_pool(name="pieces", bufs=N_BLOCKS * C_BLOCKS) as pieces,
+        tc.tile_pool(name="work", bufs=N_BLOCKS) as work,
+        tc.tile_pool(name="pieces", bufs=len(GROUPS) * C_BLOCKS) as pieces,
         tc.psum_pool(name="sums", bufs=4) as sums,
         tc.psum_pool(name="flips", bufs=3) as flips,
         tc.psum_pool(name="idle", bufs=1) as idle,
@@ -58,32 +59,41 @@ def tile_godareamodel_kernel(tc, x, rw, rb, base, offs, out):
         unused = held.tile([P, 1], F32, name="unused")
         nc.scalar.activation(unused[:], early[:], TANH)
 
-        for b in range(N_BLOCKS):
-            neurons = slice(b * P, (b + 1) * P)
-            width = P if b == 0 else C
-            for start in range(0, C, width):
-                acc = sums.tile([P, width], F32, name="acc")
-                for k in range(D_BLOCKS):
-                    nc.tensor.matmul(
-                        acc[:],
-                        rw_tile[:, k, neurons],
-                        x_tile[:, k, start : start + width],
-                        start=(k == 0),
-                        stop=(k == D_BLOCKS - 1),
-                    )
-                values = work.tile([P, width], F32, name="values")
-                nc.scalar.activation(values[:], acc[:], TANH, bias=bias[:, b * BLOCK : b * BLOCK + 1])
-                for c in range(start // P, (start + width) // P):
-                    flip = flips.tile([P, P], F32, name="flip")
-                    nc.tensor.transpose(
-                        flip[:], values[:, c * P - start : (c + 1) * P - start], identity[:]
-                    )
-                    piece = pieces.tile([P, P], F32, name="piece")
-                    nc.vector.tensor_copy(piece[:], flip[:])
+        for group in GROUPS:
+            finished = []
+            for b in group:
+                width = P if b == 0 else C
+                values = work.tile([P, C], F32, name="values")
+                for start in range(0, C, width):
+                    columns = slice(start, start + width)
+                    acc = sums.tile([P, width], F32, name="acc")
+                    for k in range(D_BLOCKS):
+                        nc.tensor.matmul(
+                            acc[:],
+                            rw_tile[:, k, b * P : (b + 1) * P],
+                            x_tile[:, k, columns],
+                            start=(k == 0),
+                            stop=(k == D_BLOCKS - 1),
+                        )
                     nc.scalar.activation(
-                        windows[c][:].indirect(offsets[:, b * P // 16 : (b + 1) * P // 16]),
-                        piece[:],
-                        COPY,
+                        values[:, columns], acc[:], TANH, bias=bias[:, b * BLOCK : b * BLOCK + 1]
                     )
+                finished.append(values)
+
+            areas = len(group) * P
+            first = group[0] * P
+            for c in range(C_BLOCKS):
+                flip = flips.tile([P, areas], F32, name="flip")
+                for i, values in enumerate(finished):
+                    nc.tensor.transpose(
+                        flip[:, i * P : (i + 1) * P], values[:, c * P : (c + 1) * P], identity[:]
+                    )
+                piece = pieces.tile([P, areas], F32, name="piece")
+                nc.vector.tensor_copy(piece[:], flip[:])
+                nc.scalar.activation(
+                    windows[c][:].indirect(offsets[:, first // 16 : (first + areas) // 16]),
+                    piece[:],
+                    COPY,
+                )
         for c in range(C_BLOCKS):
             nc.sync.dma_start(out[c * P : (c + 1) * P, :], windows[c][:])

@@ -44,7 +44,7 @@ def tile_godareamodel_kernel(tc, x, rw, rb, base, offs, out):
         make_identity(nc, identity[:])
 
         nc.sync.dma_start(x_tile[:], x.rearrange("(p k) c -> p k c", p=P))
-        nc.scalar.dma_start(rw_tile[:], rw.rearrange("(p k) n -> p k n", p=P))
+        nc.sync.dma_start(rw_tile[:], rw.rearrange("(p k) n -> p k n", p=P))
         nc.sync.dma_start(
             bias_rows[0:P:BLOCK, 0 : N_BLOCKS * BLOCK],
             rb.rearrange("o (b q i) -> q (o b) i", q=P // BLOCK, i=BLOCK),

import concourse.mybir as mybir
from concourse.masks import make_identity

P = 128
D, C, N, S = 256, 256, 384, 512
BLOCK = 32
D_BLOCKS, C_BLOCKS, N_BLOCKS = D // P, C // P, N // P
BANK = 512
GROUPS = ((0,), tuple(range(1, N_BLOCKS)))
WARM_UPS = 2

FLOPS = 2 * C * D * N

BF16, F32, U16 = mybir.dt.bfloat16, mybir.dt.float32, mybir.dt.uint16
TANH = mybir.ActivationFunctionType.Tanh
COPY = mybir.ActivationFunctionType.Copy


def tile_godareamodel_kernel(tc, x, rw, rb, base, offs, out):
    nc = tc.nc
    with (
        tc.tile_pool(name="held", bufs=1) as held,
        tc.tile_pool(name="work", bufs=N_BLOCKS) as work,
        tc.tile_pool(name="pieces", bufs=len(GROUPS) * C_BLOCKS) as pieces,
        tc.psum_pool(name="sums", bufs=4) as sums,
        tc.psum_pool(name="flips", bufs=3) as flips,
        tc.psum_pool(name="idle", bufs=1) as idle,
    ):
        bias_rows = held.tile([P, P], F32, name="bias_rows", align_bytes=64)
        nc.vector.memset(bias_rows[:], 0.0)

        zeros = held.tile([P, BANK], BF16, name="zeros")
        nc.vector.memset(zeros[:], 0.0)
        unread = idle.tile([P, BANK], F32, name="unread")
        for warm_up in range(WARM_UPS):
            nc.tensor.matmul(unread[:], zeros[:, 0:P], zeros[:], start=True, stop=True)

        x_tile = held.tile([P, D_BLOCKS, C], BF16, name="x_tile")
        rw_tile = held.tile([P, D_BLOCKS, N], BF16, name="rw_tile")
        bias = held.tile([P, P], F32, name="bias", align_bytes=64)
        offsets = held.tile([P, N // 16], U16, name="offsets")
        windows = [held.tile([P, S], F32, name=f"window{c}") for c in range(C_BLOCKS)]
        identity = held.tile([P, P], F32, name="identity")
        make_identity(nc, identity[:])

        nc.sync.dma_start(x_tile[:], x.rearrange("(p k) c -> p k c", p=P))
        nc.sync.dma_start(rw_tile[:], rw.rearrange("(p k) n -> p k n", p=P))
        nc.sync.dma_start(
            bias_rows[0:P:BLOCK, 0 : N_BLOCKS * BLOCK],
            rb.rearrange("o (b q i) -> q (o b) i", q=P // BLOCK, i=BLOCK),
        )
        nc.vector.transpose(bias[:], bias_rows[:])
        nc.sync.dma_start(offsets[:], offs)
        for c in range(C_BLOCKS):
            nc.sync.dma_start(windows[c][:], base[c * P : (c + 1) * P, :])

        early = held.tile([P, 1], F32, name="early")
        nc.gpsimd.memset(early[:], 0.0)
        unused = held.tile([P, 1], F32, name="unused")
        nc.scalar.activation(unused[:], early[:], TANH)

        for group in GROUPS:
            finished = []
            for b in group:
                width = P if b == 0 else C
                values = work.tile([P, C], F32, name="values")
                for start in range(0, C, width):
                    columns = slice(start, start + width)
                    acc = sums.tile([P, width], F32, name="acc")
                    for k in range(D_BLOCKS):
                        nc.tensor.matmul(
                            acc[:],
                            rw_tile[:, k, b * P : (b + 1) * P],
                            x_tile[:, k, columns],
                            start=(k == 0),
                            stop=(k == D_BLOCKS - 1),
                        )
                    nc.scalar.activation(
                        values[:, columns], acc[:], TANH, bias=bias[:, b * BLOCK : b * BLOCK + 1]
                    )
                finished.append(values)

            areas = len(group) * P
            first = group[0] * P
            for c in range(C_BLOCKS):
                flip = flips.tile([P, areas], F32, name="flip")
                for i, values in enumerate(finished):
                    nc.tensor.transpose(
                        flip[:, i * P : (i + 1) * P], values[:, c * P : (c + 1) * P], identity[:]
                    )
                piece = pieces.tile([P, areas], F32, name="piece")
                nc.vector.tensor_copy(piece[:], flip[:])
                nc.scalar.activation(
                    windows[c][:].indirect(offsets[:, first // 16 : (first + areas) // 16]),
                    piece[:],
                    COPY,
                )
        for c in range(C_BLOCKS):
            nc.sync.dma_start(out[c * P : (c + 1) * P, :], windows[c][:])
